import numpy as np
import ml_dtypes


def mxq(x, axis, fmt="e4m3"):
    dtype, down = {"e4m3": (ml_dtypes.float8_e4m3fn, 7), "e5m2": (ml_dtypes.float8_e5m2, 14)}[fmt]
    v = np.moveaxis(np.asarray(x, np.float32).astype(ml_dtypes.bfloat16).astype(np.float64), axis, -1)
    blocks = v.reshape(v.shape[:-1] + (-1, 32))
    amax = np.abs(blocks).max(-1, keepdims=True)
    byte = np.maximum(np.where(amax > 0, np.frexp(amax)[1] - 1 + 127, 0) - down, 1)
    scale = np.exp2(byte - 127.0)
    codes = (blocks / scale).astype(np.float32).astype(dtype).astype(np.float64)
    return np.moveaxis((codes * scale).reshape(v.shape), -1, axis)


WIDE = False


def mx_kscale(k):
    if not WIDE:
        return np.ones(k)
    levels = np.array([10, -10, 5, -5, 0])
    a = np.random.permutation(np.resize(levels, k // 512 * 4)).reshape(k // 512, 4)
    idx = np.arange(k)
    return np.exp2(a[idx // 512, idx % 128 // 32])


BF16 = ml_dtypes.bfloat16


def bf(x):
    return np.asarray(x, np.float32).astype(BF16)


def f64(x):
    return np.asarray(x).astype(np.float64)


E2M1 = np.array([0.0, 0.5, 1.0, 1.5, 2.0, 3.0, 4.0, 6.0, -0.0, -0.5, -1.0, -1.5, -2.0, -3.0, -4.0, -6.0])


def pack_weight(w, fmt):
    k, n = w.shape
    w = f64(bf(w)).reshape(k // 32, 32, n)
    amax = np.abs(w).max(1)
    if fmt == "e4m3":
        byte = np.frexp(amax)[1] - 1 + 127 - 7
    else:
        mant, ex = np.frexp(amax / 6.0)
        byte = np.where(mant > 0.5, ex, ex - 1) + 127
    byte = np.clip(np.where(amax > 0, byte, 1), 1, 254)
    scaled = (w * np.exp2(127.0 - byte)[:, None, :]).reshape(k, n).astype(np.float32)
    by_word = np.ascontiguousarray(scaled.reshape(k // 512, 128, 4, n).transpose(0, 1, 3, 2))
    if fmt == "e4m3":
        words = by_word.astype(ml_dtypes.float8_e4m3fn).view(np.uint8)
    else:
        c = by_word.astype(ml_dtypes.float4_e2m1fn).view(np.uint8) & 0xF
        words = c[..., 0::2] | (c[..., 1::2] << 4)
    return np.ascontiguousarray(words), np.ascontiguousarray(byte.astype(np.uint8).reshape(k // 512, 16, n))


def unpack_weight(words, scales, fmt):
    g, p, n, _ = words.shape
    if fmt == "e4m3":
        vals = np.ascontiguousarray(words).view(ml_dtypes.float8_e4m3fn).astype(np.float64)
    else:
        nib = np.empty((g, p, n, 4), np.uint8)
        nib[..., 0::2] = words & 0xF
        nib[..., 1::2] = words >> 4
        vals = E2M1[nib]
    vals = vals * np.repeat(np.exp2(scales.astype(np.float64) - 127.0), 8, axis=1)[..., None]
    return vals.transpose(0, 1, 3, 2).reshape(g * 512, n)

def pack4(w):
    words, scales = pack_weight(w, "e2m1")
    return words.reshape(words.shape[0], 128, -1), scales


def unpack4(words, scales):
    return unpack_weight(words.reshape(words.shape[0], 128, -1, 2), scales, "e2m1")


B, A, C, P = 64, 7, 1024, 1024
N = A * A + 1


def scramble(y):
    return y.transpose(0, 2, 1).reshape(B, N, C)


def unscramble(z):
    return z.reshape(B, C, N).transpose(0, 2, 1)


def setup_inputs():
    s = mx_kscale(C)
    z = np.random.standard_normal((B, N, C)) * 1.6 / np.sqrt(N) * s
    w = np.random.standard_normal((P, C)) * 2.0 / np.sqrt(C) / s
    words, scales = pack4(np.ascontiguousarray(w.T))
    return {"y_attn": bf(np.ascontiguousarray(unscramble(z))),
            "w_proj_words": words,
            "w_proj_scales": scales,
            "b_proj": bf(np.random.standard_normal(P) * 0.1)}


def reference(y_attn, w_proj_words, w_proj_scales, b_proj):
    z = scramble(f64(y_attn))
    return (mxq(z, 2, "e4m3") @ unpack4(w_proj_words, w_proj_scales)) + f64(b_proj)

@@ -1,0 +1,181 @@
+from contextlib import ExitStack
+
+import concourse.mybir as mybir
+from concourse.masks import make_identity
+
+BF16 = mybir.dt.bfloat16
+F32 = mybir.dt.float32
+I32 = mybir.dt.int32
+U8 = mybir.dt.uint8
+U32 = mybir.dt.uint32
+FP8X4 = mybir.dt.float8_e4m3fn_x4
+FP4X4 = mybir.dt.float4_e2m1fn_x4
+ADD = mybir.AluOpType.add
+MULT = mybir.AluOpType.mult
+
+P = 128
+IMAGES = 64
+TOKENS = 50
+CHANNELS = 1024
+FEATURES = 1024
+HALVES = 2
+HALF_CHANNELS = CHANNELS // HALVES
+HALF_ROWS = TOKENS // HALVES
+PACK = 4
+K_PASS = P * PACK
+PASSES = CHANNELS // K_PASS
+WORD = 2
+N_TILE = 512
+N_TILES = FEATURES // N_TILE
+
+GROUP = 2
+BLOCK_CHANNELS = 32
+BLOCK = BLOCK_CHANNELS * TOKENS
+BLOCKS = HALF_CHANNELS // BLOCK_CHANNELS
+RUN = 4
+CHANNEL_CUTS = (0, 128, 256, 512)
+
+FLOPS = 2 * IMAGES * TOKENS * CHANNELS * FEATURES
+
+
+def tile_attention_pa_kernel(tc, y_attn, w_proj_words, w_proj_scales, b_proj, out):
+    nc = tc.nc
+    groups = [list(range(i0, min(i0 + GROUP, HALF_ROWS))) for i0 in range(0, HALF_ROWS, GROUP)]
+    out_rows = out.rearrange("b (h i) f -> (b h) i f", h=HALVES)
+
+    with ExitStack() as ctx:
+        keep = ctx.enter_context(tc.tile_pool(name="keep", bufs=1))
+        stage = ctx.enter_context(tc.tile_pool(name="stage", bufs=3))
+        results = ctx.enter_context(tc.tile_pool(name="results", bufs=8))
+        psum_t = ctx.enter_context(tc.psum_pool(name="psum_t", bufs=4))
+        psum_o = ctx.enter_context(tc.psum_pool(name="psum_o", bufs=4))
+        ctx.enter_context(tc.manual_schedule())
+
+        y_sb = keep.tile([P, TOKENS, HALF_CHANNELS], BF16)
+        z_sb = keep.tile([P, HALF_ROWS * CHANNELS], BF16, align_bytes=64)
+        w_words = keep.tile([P, PASSES, WORD * FEATURES], U8, align_bytes=64)
+        w_scales = keep.tile([P, PASSES, FEATURES], U8, align_bytes=64)
+        bias_row = keep.tile([P, FEATURES], BF16)
+        ones = keep.tile([P, P], BF16)
+        bias_all = keep.tile([P, FEATURES], F32)
+        identity = keep.tile([P, P], F32)
+
+        nc.vector.memset(w_scales[:].bitcast(I32), 0)
+        nc.vector.memset(bias_row[:], 0.0)
+        nc.vector.memset(ones[:], 1.0)
+        make_identity(nc, identity[:])
+
+        def load_channels(c0, c1):
+            for h in range(HALVES):
+                nc.sync.dma_start(
+                    out=y_sb[h:P:HALVES, :, c0:c1],
+                    in_=y_attn[:, :, h * HALF_CHANNELS + c0 : h * HALF_CHANNELS + c1],
+                )
+
+        load_channels(CHANNEL_CUTS[0], CHANNEL_CUTS[1])
+        scale_rows = w_proj_scales.rearrange("g q n -> q g n")
+        for r in range(4):
+            nc.sync.dma_start(
+                out=w_scales[r:P:32, :, :].bitcast(I32), in_=scale_rows[r:16:4, :, :].bitcast(I32)
+            )
+        nc.sync.dma_start(
+            out=w_words[:].bitcast(I32), in_=w_proj_words.rearrange("g p n -> p g n").bitcast(I32)
+        )
+        nc.sync.dma_start(out=bias_row[0:1, :], in_=b_proj.unsqueeze(0))
+        for c0, c1 in zip(CHANNEL_CUTS[1:-1], CHANNEL_CUTS[2:]):
+            load_channels(c0, c1)
+
+        for t in range(N_TILES):
+            cols = slice(t * N_TILE, (t + 1) * N_TILE)
+            acc = psum_o.tile([P, N_TILE], F32, tag="acc")
+            nc.tensor.matmul(out=acc[:], lhsT=ones[:], rhs=bias_row[:, cols], start=True, stop=True)
+            nc.vector.tensor_copy(out=bias_all[:, cols], in_=acc[:])
+
+        def blocks_until(j):
+            rows = min((j + 1) * GROUP, HALF_ROWS)
+            return min(BLOCKS, -(-rows * CHANNELS // BLOCK))
+
+        def permute(block):
+            c0 = block * BLOCK_CHANNELS
+            src = y_sb[:, :, c0 : c0 + BLOCK_CHANNELS].rearrange("p n (c i) -> p c n i", i=RUN)
+            dst = z_sb[:, block * BLOCK : (block + 1) * BLOCK].rearrange(
+                "p (c i n) -> p c n i", i=RUN, n=TOKENS
+            )
+            if block % 2 == 0:
+                nc.scalar.copy(out=dst, in_=src)
+            else:
+                nc.gpsimd.tensor_scalar(out=dst, in0=src, scalar1=1.0, scalar2=0.0, op0=MULT, op1=ADD)
+
+        z_words = z_sb[:].bitcast(F32)
+        grouped_of = {}
+        codes_of = {}
+        scales_of = {}
+
+        def transpose_and_copy(j):
+            grouped = stage.tile([P, GROUP, PASSES, P, PACK], BF16, align_bytes=64)
+            grouped_of[j] = grouped
+            flipped_of = {}
+            for i in groups[j]:
+                flipped = psum_t.tile([P, PASSES, WORD, P], F32)
+                flipped_of[i] = flipped
+                for g in range(PASSES):
+                    first = (i * PASSES + g) * K_PASS // WORD
+                    for u in range(WORD):
+                        nc.tensor.transpose(
+                            flipped[:, g, u, :],
+                            z_words[:, first + u : first + K_PASS // WORD : WORD],
+                            identity[:],
+                        )
+            for r, i in enumerate(groups[j]):
+                nc.scalar.copy(
+                    out=grouped[:, r].bitcast(F32),
+                    in_=flipped_of[i][:].rearrange("p g u c -> p g c u"),
+                )
+
+        def quantise(j):
+            n = len(groups[j]) * PASSES * P
+            codes = stage.tile([P, GROUP * PASSES * P], U32, align_bytes=64)
+            scales = stage.tile([P, GROUP * PASSES * P], U8, align_bytes=64)
+            codes_of[j] = codes
+            scales_of[j] = scales
+            nc.vector.quantize_mx(
+                out=codes[:, 0:n].bitcast(FP8X4),
+                scales=scales[:, 0:n],
+                in_=grouped_of[j][:, 0 : len(groups[j])].rearrange("p r g c t -> p (r g c t)"),
+            )
+
+        def multiply_and_store(j):
+            result = results.tile([P, GROUP, FEATURES], F32)
+            for r in range(len(groups[j])):
+                for t in range(N_TILES):
+                    acc = psum_o.tile([P, N_TILE], F32, tag="acc")
+                    for g in range(PASSES):
+                        rows = slice((r * PASSES + g) * P, (r * PASSES + g + 1) * P)
+                        nc.tensor.matmul_mx(
+                            out=acc[:],
+                            lhsT=codes_of[j][:, rows].bitcast(FP8X4),
+                            lhsT_scale=scales_of[j][:, rows],
+                            rhs=w_words[:, g, t * WORD * N_TILE : (t + 1) * WORD * N_TILE].bitcast(FP4X4),
+                            rhs_scale=w_scales[:, g, t * N_TILE : (t + 1) * N_TILE],
+                            start=(g == 0),
+                            stop=(g == PASSES - 1),
+                        )
+                    cols = slice(t * N_TILE, (t + 1) * N_TILE)
+                    nc.vector.tensor_tensor(
+                        out=result[:, r, cols], in0=acc[:], in1=bias_all[:, cols], op=ADD
+                    )
+            i0 = groups[j][0]
+            n = len(groups[j])
+            nc.sync.dma_start(out=out_rows[:, i0 : i0 + n, :], in_=result[:, 0:n, :])
+
+        for block in range(blocks_until(1)):
+            permute(block)
+        for j in range(len(groups) + 2):
+            if j < len(groups):
+                transpose_and_copy(j)
+                for block in range(blocks_until(j + 1), blocks_until(j + 2)):
+                    permute(block)
+            if 1 <= j <= len(groups):
+                quantise(j - 1)
+            if j >= 2:
+                multiply_and_store(j - 2)

@@ -24,7 +24,9 @@ HALF_ROWS = TOKENS // HALVES
 PACK = 4
 K_PASS = P * PACK
 PASSES = CHANNELS // K_PASS
-WORD = 2
+PAIR = 2
+PLANE = HALF_ROWS * CHANNELS // PAIR
+EVEN_PAIR_TOKENS = 26
 N_TILE = 512
 N_TILES = FEATURES // N_TILE
 
@@ -33,7 +35,8 @@ BLOCK_CHANNELS = 32
 BLOCK = BLOCK_CHANNELS * TOKENS
 BLOCKS = HALF_CHANNELS // BLOCK_CHANNELS
 RUN = 4
-CHANNEL_CUTS = (0, 128, 256, 512)
+VECTOR_BLOCKS = 2
+CHANNEL_CUTS = (0, 256, 512)
 
 FLOPS = 2 * IMAGES * TOKENS * CHANNELS * FEATURES
 
@@ -46,14 +49,14 @@ def tile_attention_pa_kernel(tc, y_attn, w_proj_words, w_proj_scales, b_proj, ou
     with ExitStack() as ctx:
         keep = ctx.enter_context(tc.tile_pool(name="keep", bufs=1))
         stage = ctx.enter_context(tc.tile_pool(name="stage", bufs=3))
-        results = ctx.enter_context(tc.tile_pool(name="results", bufs=8))
+        results = ctx.enter_context(tc.tile_pool(name="results", bufs=16))
         psum_t = ctx.enter_context(tc.psum_pool(name="psum_t", bufs=4))
         psum_o = ctx.enter_context(tc.psum_pool(name="psum_o", bufs=4))
         ctx.enter_context(tc.manual_schedule())
 
         y_sb = keep.tile([P, TOKENS, HALF_CHANNELS], BF16)
-        z_sb = keep.tile([P, HALF_ROWS * CHANNELS], BF16, align_bytes=64)
-        w_words = keep.tile([P, PASSES, WORD * FEATURES], U8, align_bytes=64)
+        z_planes = keep.tile([P, PAIR, PLANE], BF16, align_bytes=64)
+        w_words = keep.tile([P, PASSES, PAIR * FEATURES], U8, align_bytes=64)
         w_scales = keep.tile([P, PASSES, FEATURES], U8, align_bytes=64)
         bias_row = keep.tile([P, FEATURES], BF16)
         ones = keep.tile([P, P], BF16)
@@ -65,12 +68,22 @@ def tile_attention_pa_kernel(tc, y_attn, w_proj_words, w_proj_scales, b_proj, ou
         nc.vector.memset(ones[:], 1.0)
         make_identity(nc, identity[:])
 
+        def slots_of(pair_parity):
+            return (0, EVEN_PAIR_TOKENS) if pair_parity == 0 else (EVEN_PAIR_TOKENS, TOKENS)
+
         def load_channels(c0, c1):
-            for h in range(HALVES):
-                nc.sync.dma_start(
-                    out=y_sb[h:P:HALVES, :, c0:c1],
-                    in_=y_attn[:, :, h * HALF_CHANNELS + c0 : h * HALF_CHANNELS + c1],
-                )
+            for pair_parity in range(PAIR):
+                slot0, slot1 = slots_of(pair_parity)
+                for e in range(PAIR):
+                    for h in range(HALVES):
+                        nc.sync.dma_start(
+                            out=y_sb[h:P:HALVES, slot0 + e : slot1 : PAIR, c0:c1],
+                            in_=y_attn[
+                                :,
+                                PAIR * pair_parity + e : TOKENS : 2 * PAIR,
+                                h * HALF_CHANNELS + c0 : h * HALF_CHANNELS + c1,
+                            ],
+                        )
 
         load_channels(CHANNEL_CUTS[0], CHANNEL_CUTS[1])
         scale_rows = w_proj_scales.rearrange("g q n -> q g n")
@@ -85,28 +98,41 @@ def tile_attention_pa_kernel(tc, y_attn, w_proj_words, w_proj_scales, b_proj, ou
         for c0, c1 in zip(CHANNEL_CUTS[1:-1], CHANNEL_CUTS[2:]):
             load_channels(c0, c1)
 
-        for t in range(N_TILES):
-            cols = slice(t * N_TILE, (t + 1) * N_TILE)
-            acc = psum_o.tile([P, N_TILE], F32, tag="acc")
-            nc.tensor.matmul(out=acc[:], lhsT=ones[:], rhs=bias_row[:, cols], start=True, stop=True)
-            nc.vector.tensor_copy(out=bias_all[:, cols], in_=acc[:])
-
         def blocks_until(j):
             rows = min((j + 1) * GROUP, HALF_ROWS)
             return min(BLOCKS, -(-rows * CHANNELS // BLOCK))
 
         def permute(block):
             c0 = block * BLOCK_CHANNELS
-            src = y_sb[:, :, c0 : c0 + BLOCK_CHANNELS].rearrange("p n (c i) -> p c n i", i=RUN)
-            dst = z_sb[:, block * BLOCK : (block + 1) * BLOCK].rearrange(
-                "p (c i n) -> p c n i", i=RUN, n=TOKENS
-            )
-            if block % 2 == 0:
-                nc.scalar.copy(out=dst, in_=src)
-            else:
-                nc.gpsimd.tensor_scalar(out=dst, in0=src, scalar1=1.0, scalar2=0.0, op0=MULT, op1=ADD)
+            values = slice(block * BLOCK // PAIR, (block + 1) * BLOCK // PAIR)
+            for channel_parity in range(PAIR):
+                for pair_parity in range(PAIR):
+                    slot0, slot1 = slots_of(pair_parity)
+                    plane = (channel_parity + pair_parity) % PAIR
+                    first = PAIR * ((HALF_ROWS * channel_parity + pair_parity) // PAIR)
+                    src = y_sb[
+                        :, slot0:slot1, c0 + channel_parity : c0 + BLOCK_CHANNELS : PAIR
+                    ].rearrange("p s (d i) -> p d s i", i=RUN)
+                    dst = z_planes[:, plane, values].rearrange(
+                        "p (d i s) -> p d s i", i=RUN, s=TOKENS
+                    )[:, :, first : first + slot1 - slot0, :]
+                    if block < VECTOR_BLOCKS:
+                        nc.vector.tensor_copy(out=dst, in_=src)
+                    elif (block - VECTOR_BLOCKS) % 2 == 0:
+                        nc.scalar.copy(out=dst, in_=src)
+                    else:
+                        nc.gpsimd.tensor_scalar(
+                            out=dst, in0=src, scalar1=1.0, scalar2=0.0, op0=MULT, op1=ADD
+                        )
 
-        z_words = z_sb[:].bitcast(F32)
+        def spread_bias():
+            for t in range(N_TILES):
+                cols = slice(t * N_TILE, (t + 1) * N_TILE)
+                acc = psum_o.tile([P, N_TILE], F32, tag="acc")
+                nc.tensor.matmul(out=acc[:], lhsT=ones[:], rhs=bias_row[:, cols], start=True, stop=True)
+                nc.vector.tensor_copy(out=bias_all[:, cols], in_=acc[:])
+
+        z_words = z_planes[:].bitcast(F32)
         grouped_of = {}
         codes_of = {}
         scales_of = {}
@@ -116,16 +142,12 @@ def tile_attention_pa_kernel(tc, y_attn, w_proj_words, w_proj_scales, b_proj, ou
             grouped_of[j] = grouped
             flipped_of = {}
             for i in groups[j]:
-                flipped = psum_t.tile([P, PASSES, WORD, P], F32)
+                flipped = psum_t.tile([P, PASSES, PAIR, P], F32)
                 flipped_of[i] = flipped
                 for g in range(PASSES):
-                    first = (i * PASSES + g) * K_PASS // WORD
-                    for u in range(WORD):
-                        nc.tensor.transpose(
-                            flipped[:, g, u, :],
-                            z_words[:, first + u : first + K_PASS // WORD : WORD],
-                            identity[:],
-                        )
+                    w0 = (i * PASSES + g) * P
+                    for u in range(PAIR):
+                        nc.tensor.transpose(flipped[:, g, u, :], z_words[:, u, w0 : w0 + P], identity[:])
             for r, i in enumerate(groups[j]):
                 nc.scalar.copy(
                     out=grouped[:, r].bitcast(F32),
@@ -145,8 +167,8 @@ def tile_attention_pa_kernel(tc, y_attn, w_proj_words, w_proj_scales, b_proj, ou
             )
 
         def multiply_and_store(j):
-            result = results.tile([P, GROUP, FEATURES], F32)
-            for r in range(len(groups[j])):
+            for r, i in enumerate(groups[j]):
+                result = results.tile([P, FEATURES], F32)
                 for t in range(N_TILES):
                     acc = psum_o.tile([P, N_TILE], F32, tag="acc")
                     for g in range(PASSES):
@@ -155,21 +177,18 @@ def tile_attention_pa_kernel(tc, y_attn, w_proj_words, w_proj_scales, b_proj, ou
                             out=acc[:],
                             lhsT=codes_of[j][:, rows].bitcast(FP8X4),
                             lhsT_scale=scales_of[j][:, rows],
-                            rhs=w_words[:, g, t * WORD * N_TILE : (t + 1) * WORD * N_TILE].bitcast(FP4X4),
+                            rhs=w_words[:, g, t * PAIR * N_TILE : (t + 1) * PAIR * N_TILE].bitcast(FP4X4),
                             rhs_scale=w_scales[:, g, t * N_TILE : (t + 1) * N_TILE],
                             start=(g == 0),
                             stop=(g == PASSES - 1),
                         )
                     cols = slice(t * N_TILE, (t + 1) * N_TILE)
-                    nc.vector.tensor_tensor(
-                        out=result[:, r, cols], in0=acc[:], in1=bias_all[:, cols], op=ADD
-                    )
-            i0 = groups[j][0]
-            n = len(groups[j])
-            nc.sync.dma_start(out=out_rows[:, i0 : i0 + n, :], in_=result[:, 0:n, :])
+                    nc.vector.tensor_tensor(out=result[:, cols], in0=acc[:], in1=bias_all[:, cols], op=ADD)
+                nc.sync.dma_start(out=out_rows[:, i, :], in_=result[:])
 
         for block in range(blocks_until(1)):
             permute(block)
+        spread_bias()
         for j in range(len(groups) + 2):
             if j < len(groups):
                 transpose_and_copy(j)

@@ -24,9 +24,7 @@ HALF_ROWS = TOKENS // HALVES
 PACK = 4
 K_PASS = P * PACK
 PASSES = CHANNELS // K_PASS
-PAIR = 2
-PLANE = HALF_ROWS * CHANNELS // PAIR
-EVEN_PAIR_TOKENS = 26
+WORD = 2
 N_TILE = 512
 N_TILES = FEATURES // N_TILE
 
@@ -35,8 +33,7 @@ BLOCK_CHANNELS = 32
 BLOCK = BLOCK_CHANNELS * TOKENS
 BLOCKS = HALF_CHANNELS // BLOCK_CHANNELS
 RUN = 4
-VECTOR_BLOCKS = 2
-CHANNEL_CUTS = (0, 256, 512)
+CHANNEL_CUTS = (0, 128, 256, 512)
 
 FLOPS = 2 * IMAGES * TOKENS * CHANNELS * FEATURES
 
@@ -55,8 +52,8 @@ def tile_attention_pa_kernel(tc, y_attn, w_proj_words, w_proj_scales, b_proj, ou
         ctx.enter_context(tc.manual_schedule())
 
         y_sb = keep.tile([P, TOKENS, HALF_CHANNELS], BF16)
-        z_planes = keep.tile([P, PAIR, PLANE], BF16, align_bytes=64)
-        w_words = keep.tile([P, PASSES, PAIR * FEATURES], U8, align_bytes=64)
+        z_sb = keep.tile([P, HALF_ROWS * CHANNELS], BF16, align_bytes=64)
+        w_words = keep.tile([P, PASSES, WORD * FEATURES], U8, align_bytes=64)
         w_scales = keep.tile([P, PASSES, FEATURES], U8, align_bytes=64)
         bias_row = keep.tile([P, FEATURES], BF16)
         ones = keep.tile([P, P], BF16)
@@ -68,22 +65,12 @@ def tile_attention_pa_kernel(tc, y_attn, w_proj_words, w_proj_scales, b_proj, ou
         nc.vector.memset(ones[:], 1.0)
         make_identity(nc, identity[:])
 
-        def slots_of(pair_parity):
-            return (0, EVEN_PAIR_TOKENS) if pair_parity == 0 else (EVEN_PAIR_TOKENS, TOKENS)
-
         def load_channels(c0, c1):
-            for pair_parity in range(PAIR):
-                slot0, slot1 = slots_of(pair_parity)
-                for e in range(PAIR):
-                    for h in range(HALVES):
-                        nc.sync.dma_start(
-                            out=y_sb[h:P:HALVES, slot0 + e : slot1 : PAIR, c0:c1],
-                            in_=y_attn[
-                                :,
-                                PAIR * pair_parity + e : TOKENS : 2 * PAIR,
-                                h * HALF_CHANNELS + c0 : h * HALF_CHANNELS + c1,
-                            ],
-                        )
+            for h in range(HALVES):
+                nc.sync.dma_start(
+                    out=y_sb[h:P:HALVES, :, c0:c1],
+                    in_=y_attn[:, :, h * HALF_CHANNELS + c0 : h * HALF_CHANNELS + c1],
+                )
 
         load_channels(CHANNEL_CUTS[0], CHANNEL_CUTS[1])
         scale_rows = w_proj_scales.rearrange("g q n -> q g n")
@@ -98,41 +85,28 @@ def tile_attention_pa_kernel(tc, y_attn, w_proj_words, w_proj_scales, b_proj, ou
         for c0, c1 in zip(CHANNEL_CUTS[1:-1], CHANNEL_CUTS[2:]):
             load_channels(c0, c1)
 
+        for t in range(N_TILES):
+            cols = slice(t * N_TILE, (t + 1) * N_TILE)
+            acc = psum_o.tile([P, N_TILE], F32, tag="acc")
+            nc.tensor.matmul(out=acc[:], lhsT=ones[:], rhs=bias_row[:, cols], start=True, stop=True)
+            nc.vector.tensor_copy(out=bias_all[:, cols], in_=acc[:])
+
         def blocks_until(j):
             rows = min((j + 1) * GROUP, HALF_ROWS)
             return min(BLOCKS, -(-rows * CHANNELS // BLOCK))
 
         def permute(block):
             c0 = block * BLOCK_CHANNELS
-            values = slice(block * BLOCK // PAIR, (block + 1) * BLOCK // PAIR)
-            for channel_parity in range(PAIR):
-                for pair_parity in range(PAIR):
-                    slot0, slot1 = slots_of(pair_parity)
-                    plane = (channel_parity + pair_parity) % PAIR
-                    first = PAIR * ((HALF_ROWS * channel_parity + pair_parity) // PAIR)
-                    src = y_sb[
-                        :, slot0:slot1, c0 + channel_parity : c0 + BLOCK_CHANNELS : PAIR
-                    ].rearrange("p s (d i) -> p d s i", i=RUN)
-                    dst = z_planes[:, plane, values].rearrange(
-                        "p (d i s) -> p d s i", i=RUN, s=TOKENS
-                    )[:, :, first : first + slot1 - slot0, :]
-                    if block < VECTOR_BLOCKS:
-                        nc.vector.tensor_copy(out=dst, in_=src)
-                    elif (block - VECTOR_BLOCKS) % 2 == 0:
-                        nc.scalar.copy(out=dst, in_=src)
-                    else:
-                        nc.gpsimd.tensor_scalar(
-                            out=dst, in0=src, scalar1=1.0, scalar2=0.0, op0=MULT, op1=ADD
-                        )
+            src = y_sb[:, :, c0 : c0 + BLOCK_CHANNELS].rearrange("p n (c i) -> p c n i", i=RUN)
+            dst = z_sb[:, block * BLOCK : (block + 1) * BLOCK].rearrange(
+                "p (c i n) -> p c n i", i=RUN, n=TOKENS
+            )
+            if block % 2 == 0:
+                nc.scalar.copy(out=dst, in_=src)
+            else:
+                nc.gpsimd.tensor_scalar(out=dst, in0=src, scalar1=1.0, scalar2=0.0, op0=MULT, op1=ADD)
 
-        def spread_bias():
-            for t in range(N_TILES):
-                cols = slice(t * N_TILE, (t + 1) * N_TILE)
-                acc = psum_o.tile([P, N_TILE], F32, tag="acc")
-                nc.tensor.matmul(out=acc[:], lhsT=ones[:], rhs=bias_row[:, cols], start=True, stop=True)
-                nc.vector.tensor_copy(out=bias_all[:, cols], in_=acc[:])
-
-        z_words = z_planes[:].bitcast(F32)
+        z_words = z_sb[:].bitcast(F32)
         grouped_of = {}
         codes_of = {}
         scales_of = {}
@@ -142,12 +116,16 @@ def tile_attention_pa_kernel(tc, y_attn, w_proj_words, w_proj_scales, b_proj, ou
             grouped_of[j] = grouped
             flipped_of = {}
             for i in groups[j]:
-                flipped = psum_t.tile([P, PASSES, PAIR, P], F32)
+                flipped = psum_t.tile([P, PASSES, WORD, P], F32)
                 flipped_of[i] = flipped
                 for g in range(PASSES):
-                    w0 = (i * PASSES + g) * P
-                    for u in range(PAIR):
-                        nc.tensor.transpose(flipped[:, g, u, :], z_words[:, u, w0 : w0 + P], identity[:])
+                    first = (i * PASSES + g) * K_PASS // WORD
+                    for u in range(WORD):
+                        nc.tensor.transpose(
+                            flipped[:, g, u, :],
+                            z_words[:, first + u : first + K_PASS // WORD : WORD],
+                            identity[:],
+                        )
             for r, i in enumerate(groups[j]):
                 nc.scalar.copy(
                     out=grouped[:, r].bitcast(F32),
@@ -177,7 +155,7 @@ def tile_attention_pa_kernel(tc, y_attn, w_proj_words, w_proj_scales, b_proj, ou
                             out=acc[:],
                             lhsT=codes_of[j][:, rows].bitcast(FP8X4),
                             lhsT_scale=scales_of[j][:, rows],
-                            rhs=w_words[:, g, t * PAIR * N_TILE : (t + 1) * PAIR * N_TILE].bitcast(FP4X4),
+                            rhs=w_words[:, g, t * WORD * N_TILE : (t + 1) * WORD * N_TILE].bitcast(FP4X4),
                             rhs_scale=w_scales[:, g, t * N_TILE : (t + 1) * N_TILE],
                             start=(g == 0),
                             stop=(g == PASSES - 1),
@@ -185,16 +163,20 @@ def tile_attention_pa_kernel(tc, y_attn, w_proj_words, w_proj_scales, b_proj, ou
                     cols = slice(t * N_TILE, (t + 1) * N_TILE)
                     nc.vector.tensor_tensor(out=result[:, cols], in0=acc[:], in1=bias_all[:, cols], op=ADD)
                 nc.sync.dma_start(out=out_rows[:, i, :], in_=result[:])
+                if r == 0 and j + 1 < len(groups):
+                    quantise(j + 1)
 
-        for block in range(blocks_until(1)):
-            permute(block)
-        spread_bias()
-        for j in range(len(groups) + 2):
+        def transpose_ahead(j):
             if j < len(groups):
                 transpose_and_copy(j)
                 for block in range(blocks_until(j + 1), blocks_until(j + 2)):
                     permute(block)
-            if 1 <= j <= len(groups):
-                quantise(j - 1)
-            if j >= 2:
-                multiply_and_store(j - 2)
+
+        for block in range(blocks_until(1)):
+            permute(block)
+        transpose_ahead(0)
+        transpose_ahead(1)
+        quantise(0)
+        for j in range(len(groups)):
+            multiply_and_store(j)
+            transpose_ahead(j + 2)

@@ -11,7 +11,6 @@ U32 = mybir.dt.uint32
 FP8X4 = mybir.dt.float8_e4m3fn_x4
 FP4X4 = mybir.dt.float4_e2m1fn_x4
 ADD = mybir.AluOpType.add
-MULT = mybir.AluOpType.mult
 
 P = 128
 IMAGES = 64
@@ -29,7 +28,7 @@ N_TILE = 512
 N_TILES = FEATURES // N_TILE
 
 GROUP = 2
-BLOCK_CHANNELS = 32
+BLOCK_CHANNELS = 16
 BLOCK = BLOCK_CHANNELS * TOKENS
 BLOCKS = HALF_CHANNELS // BLOCK_CHANNELS
 RUN = 4
@@ -101,10 +100,10 @@ def tile_attention_pa_kernel(tc, y_attn, w_proj_words, w_proj_scales, b_proj, ou
             dst = z_sb[:, block * BLOCK : (block + 1) * BLOCK].rearrange(
                 "p (c i n) -> p c n i", i=RUN, n=TOKENS
             )
-            if block % 2 == 0:
+            if block % 4 != 3:
                 nc.scalar.copy(out=dst, in_=src)
             else:
-                nc.gpsimd.tensor_scalar(out=dst, in0=src, scalar1=1.0, scalar2=0.0, op0=MULT, op1=ADD)
+                nc.vector.tensor_copy(out=dst, in_=src)
 
         z_words = z_sb[:].bitcast(F32)
         grouped_of = {}

@@ -11,6 +11,7 @@ U32 = mybir.dt.uint32
 FP8X4 = mybir.dt.float8_e4m3fn_x4
 FP4X4 = mybir.dt.float4_e2m1fn_x4
 ADD = mybir.AluOpType.add
+MULT = mybir.AluOpType.mult
 
 P = 128
 IMAGES = 64
@@ -26,11 +27,17 @@ PASSES = CHANNELS // K_PASS
 WORD = 2
 N_TILE = 512
 N_TILES = FEATURES // N_TILE
+A_SLOTS = 26
+B_SLOTS = 24
+PLANE = HALF_ROWS * CHANNELS // WORD + 32
+ROW_QUADS = CHANNELS // PACK
+PAIR_QUADS = 25
 
-GROUP = 2
-BLOCK_CHANNELS = 16
-BLOCK = BLOCK_CHANNELS * TOKENS
-BLOCKS = HALF_CHANNELS // BLOCK_CHANNELS
+ROW_ORDER = tuple(range(1, HALF_ROWS)) + (0,)
+GROUP_SIZES = (2,) * 12 + (1,)
+MAX_GROUP = max(GROUP_SIZES)
+QUANT_ROWS = 2
+BLOCK_CUTS = tuple(range(0, 513, 32))
 RUN = 4
 CHANNEL_CUTS = (0, 128, 256, 512)
 
@@ -39,19 +46,28 @@ FLOPS = 2 * IMAGES * TOKENS * CHANNELS * FEATURES
 
 def tile_attention_pa_kernel(tc, y_attn, w_proj_words, w_proj_scales, b_proj, out):
     nc = tc.nc
-    groups = [list(range(i0, min(i0 + GROUP, HALF_ROWS))) for i0 in range(0, HALF_ROWS, GROUP)]
+    groups = []
+    for size in GROUP_SIZES:
+        first = sum(len(g) for g in groups)
+        groups.append(list(ROW_ORDER[first : first + size]))
+    assert sorted(i for g in groups for i in g) == list(range(HALF_ROWS))
     out_rows = out.rearrange("b (h i) f -> (b h) i f", h=HALVES)
+    y_flat = y_attn.rearrange("b n c -> b (n c)")
 
     with ExitStack() as ctx:
         keep = ctx.enter_context(tc.tile_pool(name="keep", bufs=1))
         stage = ctx.enter_context(tc.tile_pool(name="stage", bufs=3))
-        results = ctx.enter_context(tc.tile_pool(name="results", bufs=16))
+        results = ctx.enter_context(tc.tile_pool(name="results", bufs=12))
         psum_t = ctx.enter_context(tc.psum_pool(name="psum_t", bufs=4))
         psum_o = ctx.enter_context(tc.psum_pool(name="psum_o", bufs=4))
         ctx.enter_context(tc.manual_schedule())
 
-        y_sb = keep.tile([P, TOKENS, HALF_CHANNELS], BF16)
-        z_sb = keep.tile([P, HALF_ROWS * CHANNELS], BF16, align_bytes=64)
+        y_pieces = []
+        for c0, c1 in zip(CHANNEL_CUTS[:-1], CHANNEL_CUTS[1:]):
+            piece = keep.tile([P, TOKENS, c1 - c0], BF16, name="y_piece_%d" % c0)
+            y_pieces.append(piece)
+        y_first = keep.tile([P, WORD, 16, WORD], BF16)
+        z_sb = keep.tile([P, WORD, PLANE], BF16, align_bytes=64)
         w_words = keep.tile([P, PASSES, WORD * FEATURES], U8, align_bytes=64)
         w_scales = keep.tile([P, PASSES, FEATURES], U8, align_bytes=64)
         bias_row = keep.tile([P, FEATURES], BF16)
@@ -64,14 +80,25 @@ def tile_attention_pa_kernel(tc, y_attn, w_proj_words, w_proj_scales, b_proj, ou
         nc.vector.memset(ones[:], 1.0)
         make_identity(nc, identity[:])
 
-        def load_channels(c0, c1):
+        def load_channels(piece):
+            c0, c1 = CHANNEL_CUTS[piece], CHANNEL_CUTS[piece + 1]
             for h in range(HALVES):
-                nc.sync.dma_start(
-                    out=y_sb[h:P:HALVES, :, c0:c1],
-                    in_=y_attn[:, :, h * HALF_CHANNELS + c0 : h * HALF_CHANNELS + c1],
+                start = h * HALF_CHANNELS + c0
+                shifted = y_flat[:, WORD * CHANNELS + start + 1 : (TOKENS - 1) * CHANNELS + start + 1].rearrange(
+                    "b (n c) -> b n c", c=CHANNELS
                 )
+                for e in range(WORD):
+                    nc.sync.dma_start(
+                        out=y_pieces[piece][h:P:HALVES, e:A_SLOTS:WORD, :],
+                        in_=y_attn[:, e:TOKENS:PACK, start : start + c1 - c0],
+                    )
+                for e in range(WORD):
+                    nc.sync.dma_start(
+                        out=y_pieces[piece][h:P:HALVES, A_SLOTS + e : TOKENS : WORD, :],
+                        in_=shifted[:, e : TOKENS - 3 : PACK, 0 : c1 - c0],
+                    )
 
-        load_channels(CHANNEL_CUTS[0], CHANNEL_CUTS[1])
+        load_channels(0)
         scale_rows = w_proj_scales.rearrange("g q n -> q g n")
         for r in range(4):
             nc.sync.dma_start(
@@ -81,8 +108,14 @@ def tile_attention_pa_kernel(tc, y_attn, w_proj_words, w_proj_scales, b_proj, ou
             out=w_words[:].bitcast(I32), in_=w_proj_words.rearrange("g p n -> p g n").bitcast(I32)
         )
         nc.sync.dma_start(out=bias_row[0:1, :], in_=b_proj.unsqueeze(0))
-        for c0, c1 in zip(CHANNEL_CUTS[1:-1], CHANNEL_CUTS[2:]):
-            load_channels(c0, c1)
+        for piece in range(1, len(y_pieces)):
+            load_channels(piece)
+        for h in range(HALVES):
+            for e in range(WORD):
+                nc.sync.dma_start(
+                    out=y_first[h:P:HALVES, e, 0 : B_SLOTS // WORD, :],
+                    in_=y_attn[:, WORD + e : TOKENS : PACK, h * HALF_CHANNELS : h * HALF_CHANNELS + WORD],
+                )
 
         for t in range(N_TILES):
             cols = slice(t * N_TILE, (t + 1) * N_TILE)
@@ -90,60 +123,78 @@ def tile_attention_pa_kernel(tc, y_attn, w_proj_words, w_proj_scales, b_proj, ou
             nc.tensor.matmul(out=acc[:], lhsT=ones[:], rhs=bias_row[:, cols], start=True, stop=True)
             nc.vector.tensor_copy(out=bias_all[:, cols], in_=acc[:])
 
+        blocks = list(zip(BLOCK_CUTS[:-1], BLOCK_CUTS[1:]))
+
         def blocks_until(j):
-            rows = min((j + 1) * GROUP, HALF_ROWS)
-            return min(BLOCKS, -(-rows * CHANNELS // BLOCK))
+            rows = max(i for g in groups[: j + 1] for i in g) + 1
+            channels = WORD * ((rows * ROW_QUADS - 1) // PAIR_QUADS + 1)
+            return sum(1 for c0, c1 in blocks if c0 < channels)
+
+        def copy_on(engine, dst, src):
+            if engine == "vector":
+                nc.vector.tensor_copy(out=dst, in_=src)
+            elif engine == "gpsimd":
+                nc.gpsimd.tensor_scalar(out=dst, in0=src, scalar1=1.0, scalar2=0.0, op0=MULT, op1=ADD)
+            else:
+                nc.scalar.copy(out=dst, in_=src)
 
         def permute(block):
-            c0 = block * BLOCK_CHANNELS
-            src = y_sb[:, :, c0 : c0 + BLOCK_CHANNELS].rearrange("p n (c i) -> p c n i", i=RUN)
-            dst = z_sb[:, block * BLOCK : (block + 1) * BLOCK].rearrange(
-                "p (c i n) -> p c n i", i=RUN, n=TOKENS
-            )
-            if block % 4 != 3:
-                nc.scalar.copy(out=dst, in_=src)
-            else:
-                nc.vector.tensor_copy(out=dst, in_=src)
+            c0, c1 = blocks[block]
+            piece = max(k for k in range(len(y_pieces)) if CHANNEL_CUTS[k] <= c0)
+            base = CHANNEL_CUTS[piece]
+            columns = y_pieces[piece][:, :, c0 - base : c1 - base].rearrange("p m (c i q) -> p c m i q", i=RUN, q=WORD)
+            for parity in range(WORD):
+                first = B_SLOTS * parity + TOKENS * (c0 // WORD)
+                dst = z_sb[:, parity, first : first + TOKENS * ((c1 - c0) // WORD)].rearrange(
+                    "p (c i m) -> p c m i", i=RUN, m=TOKENS
+                )
+                copy_on("vector" if (2 * block + parity) % 4 == 3 else "scalar", dst, columns[:, :, :, :, parity])
 
-        z_words = z_sb[:].bitcast(F32)
+        z_words = z_sb[:].rearrange("p u f -> p (u f)").bitcast(F32)
         grouped_of = {}
         codes_of = {}
         scales_of = {}
 
         def transpose_and_copy(j):
-            grouped = stage.tile([P, GROUP, PASSES, P, PACK], BF16, align_bytes=64)
+            grouped = stage.tile([P, MAX_GROUP, PASSES, P, PACK], BF16, align_bytes=64)
+            codes = stage.tile([P, MAX_GROUP * PASSES * P], U32, align_bytes=64)
+            scales = stage.tile([P, MAX_GROUP * PASSES * P], U8, align_bytes=64)
             grouped_of[j] = grouped
+            codes_of[j] = codes
+            scales_of[j] = scales
             flipped_of = {}
             for i in groups[j]:
+                if i == 0:
+                    nc.scalar.copy(
+                        out=z_sb[:, 1, 0:B_SLOTS].rearrange("p (k e) -> p k e", e=WORD),
+                        in_=y_first[:, :, 0 : B_SLOTS // WORD, 0].rearrange("p e k -> p k e"),
+                    )
                 flipped = psum_t.tile([P, PASSES, WORD, P], F32)
                 flipped_of[i] = flipped
                 for g in range(PASSES):
-                    first = (i * PASSES + g) * K_PASS // WORD
                     for u in range(WORD):
-                        nc.tensor.transpose(
-                            flipped[:, g, u, :],
-                            z_words[:, first + u : first + K_PASS // WORD : WORD],
-                            identity[:],
-                        )
+                        first = u * (PLANE // WORD) + (i * PASSES + g) * P
+                        nc.tensor.transpose(flipped[:, g, u, :], z_words[:, first : first + P], identity[:])
             for r, i in enumerate(groups[j]):
                 nc.scalar.copy(
                     out=grouped[:, r].bitcast(F32),
                     in_=flipped_of[i][:].rearrange("p g u c -> p g c u"),
                 )
 
-        def quantise(j):
-            n = len(groups[j]) * PASSES * P
-            codes = stage.tile([P, GROUP * PASSES * P], U32, align_bytes=64)
-            scales = stage.tile([P, GROUP * PASSES * P], U8, align_bytes=64)
-            codes_of[j] = codes
-            scales_of[j] = scales
+        def quantise(j, r0):
+            rows = min(QUANT_ROWS, len(groups[j]) - r0)
+            cols = slice(r0 * PASSES * P, (r0 + rows) * PASSES * P)
             nc.vector.quantize_mx(
-                out=codes[:, 0:n].bitcast(FP8X4),
-                scales=scales[:, 0:n],
-                in_=grouped_of[j][:, 0 : len(groups[j])].rearrange("p r g c t -> p (r g c t)"),
+                out=codes_of[j][:, cols].bitcast(FP8X4),
+                scales=scales_of[j][:, cols],
+                in_=grouped_of[j][:, r0 : r0 + rows].rearrange("p r g c t -> p (r g c t)"),
             )
 
         def multiply_and_store(j):
+            pending = []
+            if j + 1 < len(groups):
+                pending = list(range(0, len(groups[j + 1]), QUANT_ROWS))
+            last = len(groups[j]) - 1
             for r, i in enumerate(groups[j]):
                 result = results.tile([P, FEATURES], F32)
                 for t in range(N_TILES):
@@ -162,8 +213,11 @@ def tile_attention_pa_kernel(tc, y_attn, w_proj_words, w_proj_scales, b_proj, ou
                     cols = slice(t * N_TILE, (t + 1) * N_TILE)
                     nc.vector.tensor_tensor(out=result[:, cols], in0=acc[:], in1=bias_all[:, cols], op=ADD)
                 nc.sync.dma_start(out=out_rows[:, i, :], in_=result[:])
-                if r == 0 and j + 1 < len(groups):
-                    quantise(j + 1)
+                if pending and (r % 2 == 0 or r == last):
+                    quantise(j + 1, pending.pop(0))
+                if r == last:
+                    for r0 in pending:
+                        quantise(j + 1, r0)
 
         def transpose_ahead(j):
             if j < len(groups):
@@ -175,7 +229,8 @@ def tile_attention_pa_kernel(tc, y_attn, w_proj_words, w_proj_scales, b_proj, ou
             permute(block)
         transpose_ahead(0)
         transpose_ahead(1)
-        quantise(0)
+        for r0 in range(0, len(groups[0]), QUANT_ROWS):
+            quantise(0, r0)
         for j in range(len(groups)):
             multiply_and_store(j)
             transpose_ahead(j + 2)

@@ -148,7 +148,14 @@ def tile_attention_pa_kernel(tc, y_attn, w_proj_words, w_proj_scales, b_proj, ou
                 dst = z_sb[:, parity, first : first + TOKENS * ((c1 - c0) // WORD)].rearrange(
                     "p (c i m) -> p c m i", i=RUN, m=TOKENS
                 )
-                copy_on("vector" if (2 * block + parity) % 4 == 3 else "scalar", dst, columns[:, :, :, :, parity])
+                engine = "gpsimd" if parity == 1 else "scalar"
+                src = columns[:, :, :, :, parity]
+                if engine == "gpsimd":
+                    half = src.shape[1] // 2
+                    copy_on(engine, dst[:, 0:half], src[:, 0:half])
+                    copy_on(engine, dst[:, half:], src[:, half:])
+                else:
+                    copy_on(engine, dst, src)
 
         z_words = z_sb[:].rearrange("p u f -> p (u f)").bitcast(F32)
         grouped_of = {}

@@ -29,35 +29,45 @@ N_TILE = 512
 N_TILES = FEATURES // N_TILE
 A_SLOTS = 26
 B_SLOTS = 24
-PLANE = HALF_ROWS * CHANNELS // WORD + 32
+PLANE = HALF_ROWS * CHANNELS // WORD
 ROW_QUADS = CHANNELS // PACK
 PAIR_QUADS = 25
-
-ROW_ORDER = tuple(range(1, HALF_ROWS)) + (0,)
-GROUP_SIZES = (2,) * 12 + (1,)
-MAX_GROUP = max(GROUP_SIZES)
-QUANT_ROWS = 2
-BLOCK_CUTS = tuple(range(0, 513, 32))
 RUN = 4
+STEP = RUN * WORD
 CHANNEL_CUTS = (0, 128, 256, 512)
+PAIR = 2
+PARTS = (
+    (0, 0, 0, A_SLOTS, 0),
+    (0, 1, A_SLOTS, B_SLOTS, A_SLOTS),
+    (1, 1, 0, A_SLOTS, B_SLOTS),
+    (1, 0, A_SLOTS, B_SLOTS, 0),
+)
 
 FLOPS = 2 * IMAGES * TOKENS * CHANNELS * FEATURES
 
 
 def tile_attention_pa_kernel(tc, y_attn, w_proj_words, w_proj_scales, b_proj, out):
     nc = tc.nc
-    groups = []
-    for size in GROUP_SIZES:
-        first = sum(len(g) for g in groups)
-        groups.append(list(ROW_ORDER[first : first + size]))
-    assert sorted(i for g in groups for i in g) == list(range(HALF_ROWS))
+    pairs = [list(range(i, min(i + PAIR, HALF_ROWS))) for i in range(0, HALF_ROWS, PAIR)]
     out_rows = out.rearrange("b (h i) f -> (b h) i f", h=HALVES)
-    y_flat = y_attn.rearrange("b n c -> b (n c)")
+
+    def channels_until(row):
+        if row < 0:
+            return 0
+        need = WORD * (((row + 1) * ROW_QUADS - 1) // PAIR_QUADS + 1)
+        return min(HALF_CHANNELS, -(-need // STEP) * STEP)
+
+    def piece_of(row):
+        last = channels_until(row) - 1
+        return max(k for k in range(len(CHANNEL_CUTS) - 1) if CHANNEL_CUTS[k] <= last)
+
+    def is_late(q):
+        return q > 0 and piece_of(pairs[q][-1]) > piece_of(pairs[q - 1][-1])
 
     with ExitStack() as ctx:
         keep = ctx.enter_context(tc.tile_pool(name="keep", bufs=1))
-        stage = ctx.enter_context(tc.tile_pool(name="stage", bufs=3))
-        results = ctx.enter_context(tc.tile_pool(name="results", bufs=12))
+        stage = ctx.enter_context(tc.tile_pool(name="stage", bufs=4))
+        results = ctx.enter_context(tc.tile_pool(name="results", bufs=8))
         psum_t = ctx.enter_context(tc.psum_pool(name="psum_t", bufs=4))
         psum_o = ctx.enter_context(tc.psum_pool(name="psum_o", bufs=4))
         ctx.enter_context(tc.manual_schedule())
@@ -66,38 +76,36 @@ def tile_attention_pa_kernel(tc, y_attn, w_proj_words, w_proj_scales, b_proj, ou
         for c0, c1 in zip(CHANNEL_CUTS[:-1], CHANNEL_CUTS[1:]):
             piece = keep.tile([P, TOKENS, c1 - c0], BF16, name="y_piece_%d" % c0)
             y_pieces.append(piece)
-        y_first = keep.tile([P, WORD, 16, WORD], BF16)
         z_sb = keep.tile([P, WORD, PLANE], BF16, align_bytes=64)
         w_words = keep.tile([P, PASSES, WORD * FEATURES], U8, align_bytes=64)
         w_scales = keep.tile([P, PASSES, FEATURES], U8, align_bytes=64)
         bias_row = keep.tile([P, FEATURES], BF16)
         ones = keep.tile([P, P], BF16)
+        warm = keep.tile([P, WORD], BF16)
         bias_all = keep.tile([P, FEATURES], F32)
         identity = keep.tile([P, P], F32)
 
-        nc.vector.memset(w_scales[:].bitcast(I32), 0)
         nc.vector.memset(bias_row[:], 0.0)
+        nc.vector.memset(w_scales[:].bitcast(I32), 0)
         nc.vector.memset(ones[:], 1.0)
         make_identity(nc, identity[:])
 
         def load_channels(piece):
             c0, c1 = CHANNEL_CUTS[piece], CHANNEL_CUTS[piece + 1]
             for h in range(HALVES):
-                start = h * HALF_CHANNELS + c0
-                shifted = y_flat[:, WORD * CHANNELS + start + 1 : (TOKENS - 1) * CHANNELS + start + 1].rearrange(
-                    "b (n c) -> b n c", c=CHANNELS
-                )
+                cols = slice(h * HALF_CHANNELS + c0, h * HALF_CHANNELS + c1)
                 for e in range(WORD):
                     nc.sync.dma_start(
-                        out=y_pieces[piece][h:P:HALVES, e:A_SLOTS:WORD, :],
-                        in_=y_attn[:, e:TOKENS:PACK, start : start + c1 - c0],
+                        out=y_pieces[piece][h:P:HALVES, e:A_SLOTS:WORD, :], in_=y_attn[:, e:TOKENS:PACK, cols]
                     )
                 for e in range(WORD):
                     nc.sync.dma_start(
                         out=y_pieces[piece][h:P:HALVES, A_SLOTS + e : TOKENS : WORD, :],
-                        in_=shifted[:, e : TOKENS - 3 : PACK, 0 : c1 - c0],
+                        in_=y_attn[:, WORD + e : TOKENS : PACK, cols],
                     )
 
+        nc.scalar.dma_start(out=bias_row[0:1, :], in_=b_proj.unsqueeze(0))
+        nc.scalar.copy(out=warm[:], in_=ones[:, 0:WORD])
         load_channels(0)
         scale_rows = w_proj_scales.rearrange("g q n -> q g n")
         for r in range(4):
@@ -107,28 +115,14 @@ def tile_attention_pa_kernel(tc, y_attn, w_proj_words, w_proj_scales, b_proj, ou
         nc.sync.dma_start(
             out=w_words[:].bitcast(I32), in_=w_proj_words.rearrange("g p n -> p g n").bitcast(I32)
         )
-        nc.sync.dma_start(out=bias_row[0:1, :], in_=b_proj.unsqueeze(0))
         for piece in range(1, len(y_pieces)):
             load_channels(piece)
-        for h in range(HALVES):
-            for e in range(WORD):
-                nc.sync.dma_start(
-                    out=y_first[h:P:HALVES, e, 0 : B_SLOTS // WORD, :],
-                    in_=y_attn[:, WORD + e : TOKENS : PACK, h * HALF_CHANNELS : h * HALF_CHANNELS + WORD],
-                )
 
         for t in range(N_TILES):
             cols = slice(t * N_TILE, (t + 1) * N_TILE)
             acc = psum_o.tile([P, N_TILE], F32, tag="acc")
             nc.tensor.matmul(out=acc[:], lhsT=ones[:], rhs=bias_row[:, cols], start=True, stop=True)
             nc.vector.tensor_copy(out=bias_all[:, cols], in_=acc[:])
-
-        blocks = list(zip(BLOCK_CUTS[:-1], BLOCK_CUTS[1:]))
-
-        def blocks_until(j):
-            rows = max(i for g in groups[: j + 1] for i in g) + 1
-            channels = WORD * ((rows * ROW_QUADS - 1) // PAIR_QUADS + 1)
-            return sum(1 for c0, c1 in blocks if c0 < channels)
 
         def copy_on(engine, dst, src):
             if engine == "vector":
@@ -138,106 +132,123 @@ def tile_attention_pa_kernel(tc, y_attn, w_proj_words, w_proj_scales, b_proj, ou
             else:
                 nc.scalar.copy(out=dst, in_=src)
 
-        def permute(block):
-            c0, c1 = blocks[block]
-            piece = max(k for k in range(len(y_pieces)) if CHANNEL_CUTS[k] <= c0)
-            base = CHANNEL_CUTS[piece]
-            columns = y_pieces[piece][:, :, c0 - base : c1 - base].rearrange("p m (c i q) -> p c m i q", i=RUN, q=WORD)
-            for parity in range(WORD):
-                first = B_SLOTS * parity + TOKENS * (c0 // WORD)
-                dst = z_sb[:, parity, first : first + TOKENS * ((c1 - c0) // WORD)].rearrange(
-                    "p (c i m) -> p c m i", i=RUN, m=TOKENS
-                )
-                engine = "gpsimd" if parity == 1 else "scalar"
-                src = columns[:, :, :, :, parity]
-                if engine == "gpsimd":
-                    half = src.shape[1] // 2
-                    copy_on(engine, dst[:, 0:half], src[:, 0:half])
-                    copy_on(engine, dst[:, half:], src[:, half:])
-                else:
-                    copy_on(engine, dst, src)
+        def permute(row):
+            lo, hi = channels_until(row - 1), channels_until(row)
+            for piece in range(len(y_pieces)):
+                base = CHANNEL_CUTS[piece]
+                c0, c1 = max(lo, base), min(hi, CHANNEL_CUTS[piece + 1])
+                if c0 >= c1:
+                    continue
+                for plane, parity, slot, slots, place in PARTS:
+                    src = y_pieces[piece][:, slot : slot + slots, c0 - base : c1 - base].rearrange(
+                        "p m (c i q) -> p c m i q", i=RUN, q=WORD
+                    )
+                    dst = z_sb[:, plane, TOKENS * (c0 // WORD) : TOKENS * (c1 // WORD)].rearrange(
+                        "p (c i m) -> p c m i", i=RUN, m=TOKENS
+                    )
+                    engine = (("scalar" if (plane, parity) == (1, 0) else "vector") if piece == 0 else ("scalar" if plane == 0 else "gpsimd"))
+                    copy_on(engine, dst[:, :, place : place + slots, :], src[:, :, :, :, parity])
 
         z_words = z_sb[:].rearrange("p u f -> p (u f)").bitcast(F32)
+        flipped_of = {}
         grouped_of = {}
         codes_of = {}
         scales_of = {}
 
-        def transpose_and_copy(j):
-            grouped = stage.tile([P, MAX_GROUP, PASSES, P, PACK], BF16, align_bytes=64)
-            codes = stage.tile([P, MAX_GROUP * PASSES * P], U32, align_bytes=64)
-            scales = stage.tile([P, MAX_GROUP * PASSES * P], U8, align_bytes=64)
-            grouped_of[j] = grouped
-            codes_of[j] = codes
-            scales_of[j] = scales
-            flipped_of = {}
-            for i in groups[j]:
-                if i == 0:
-                    nc.scalar.copy(
-                        out=z_sb[:, 1, 0:B_SLOTS].rearrange("p (k e) -> p k e", e=WORD),
-                        in_=y_first[:, :, 0 : B_SLOTS // WORD, 0].rearrange("p e k -> p k e"),
-                    )
-                flipped = psum_t.tile([P, PASSES, WORD, P], F32)
-                flipped_of[i] = flipped
-                for g in range(PASSES):
-                    for u in range(WORD):
-                        first = u * (PLANE // WORD) + (i * PASSES + g) * P
-                        nc.tensor.transpose(flipped[:, g, u, :], z_words[:, first : first + P], identity[:])
-            for r, i in enumerate(groups[j]):
-                nc.scalar.copy(
-                    out=grouped[:, r].bitcast(F32),
-                    in_=flipped_of[i][:].rearrange("p g u c -> p g c u"),
-                )
+        def transpose(row):
+            flipped = psum_t.tile([P, PASSES, WORD, P], F32)
+            flipped_of[row] = flipped
+            for g in range(PASSES):
+                for u in range(WORD):
+                    first = u * (PLANE // WORD) + (row * PASSES + g) * P
+                    nc.tensor.transpose(flipped[:, g, u, :], z_words[:, first : first + P], identity[:])
 
-        def quantise(j, r0):
-            rows = min(QUANT_ROWS, len(groups[j]) - r0)
-            cols = slice(r0 * PASSES * P, (r0 + rows) * PASSES * P)
-            nc.vector.quantize_mx(
-                out=codes_of[j][:, cols].bitcast(FP8X4),
-                scales=scales_of[j][:, cols],
-                in_=grouped_of[j][:, r0 : r0 + rows].rearrange("p r g c t -> p (r g c t)"),
+        def copy_out(row):
+            q, r = divmod(row, PAIR)
+            if r == 0:
+                grouped = stage.tile([P, PAIR, PASSES, P, PACK], BF16, align_bytes=64)
+                codes = stage.tile([P, PAIR * PASSES * P], U32, align_bytes=64)
+                scales = stage.tile([P, PAIR * PASSES * P], U8, align_bytes=64)
+                grouped_of[q] = grouped
+                codes_of[q] = codes
+                scales_of[q] = scales
+            nc.scalar.copy(
+                out=grouped_of[q][:, r].bitcast(F32), in_=flipped_of[row][:].rearrange("p g u c -> p g c u")
             )
 
-        def multiply_and_store(j):
-            pending = []
-            if j + 1 < len(groups):
-                pending = list(range(0, len(groups[j + 1]), QUANT_ROWS))
-            last = len(groups[j]) - 1
-            for r, i in enumerate(groups[j]):
-                result = results.tile([P, FEATURES], F32)
-                for t in range(N_TILES):
-                    acc = psum_o.tile([P, N_TILE], F32, tag="acc")
-                    for g in range(PASSES):
-                        rows = slice((r * PASSES + g) * P, (r * PASSES + g + 1) * P)
-                        nc.tensor.matmul_mx(
-                            out=acc[:],
-                            lhsT=codes_of[j][:, rows].bitcast(FP8X4),
-                            lhsT_scale=scales_of[j][:, rows],
-                            rhs=w_words[:, g, t * WORD * N_TILE : (t + 1) * WORD * N_TILE].bitcast(FP4X4),
-                            rhs_scale=w_scales[:, g, t * N_TILE : (t + 1) * N_TILE],
-                            start=(g == 0),
-                            stop=(g == PASSES - 1),
-                        )
-                    cols = slice(t * N_TILE, (t + 1) * N_TILE)
-                    nc.vector.tensor_tensor(out=result[:, cols], in0=acc[:], in1=bias_all[:, cols], op=ADD)
-                nc.sync.dma_start(out=out_rows[:, i, :], in_=result[:])
-                if pending and (r % 2 == 0 or r == last):
-                    quantise(j + 1, pending.pop(0))
-                if r == last:
-                    for r0 in pending:
-                        quantise(j + 1, r0)
+        def quantise(rows):
+            q, r0 = divmod(rows[0], PAIR)
+            cols = slice(r0 * PASSES * P, (r0 + len(rows)) * PASSES * P)
+            nc.vector.quantize_mx(
+                out=codes_of[q][:, cols].bitcast(FP8X4),
+                scales=scales_of[q][:, cols],
+                in_=grouped_of[q][:, r0 : r0 + len(rows)].rearrange("p r g c t -> p (r g c t)"),
+            )
 
-        def transpose_ahead(j):
-            if j < len(groups):
-                transpose_and_copy(j)
-                for block in range(blocks_until(j + 1), blocks_until(j + 2)):
-                    permute(block)
+        transposes_after = {}
+        quantise_after = {}
+        for q in range(PAIR, len(pairs)):
+            first = pairs[q][0]
+            if is_late(q):
+                transposes_after.setdefault(first - 2, []).append(q)
+                for r, row in enumerate(pairs[q]):
+                    quantise_after.setdefault((first - 1, r), []).append([row])
+            else:
+                transposes_after.setdefault(first - 3, []).append(q)
+                quantise_after.setdefault((first - 2, N_TILES - 1), []).append(pairs[q])
 
-        for block in range(blocks_until(1)):
-            permute(block)
-        transpose_ahead(0)
-        transpose_ahead(1)
-        for r0 in range(0, len(groups[0]), QUANT_ROWS):
-            quantise(0, r0)
-        for j in range(len(groups)):
-            multiply_and_store(j)
-            transpose_ahead(j + 2)
+        result_of = {}
+
+        def multiply_and_store(row):
+            q, r = divmod(row, PAIR)
+            if r == 0:
+                result = results.tile([P, PAIR, FEATURES], F32)
+                result_of[q] = result
+            result = result_of[q]
+            for t in range(N_TILES):
+                acc = psum_o.tile([P, N_TILE], F32, tag="acc")
+                for g in range(PASSES):
+                    cols = slice((r * PASSES + g) * P, (r * PASSES + g + 1) * P)
+                    nc.tensor.matmul_mx(
+                        out=acc[:],
+                        lhsT=codes_of[q][:, cols].bitcast(FP8X4),
+                        lhsT_scale=scales_of[q][:, cols],
+                        rhs=w_words[:, g, t * WORD * N_TILE : (t + 1) * WORD * N_TILE].bitcast(FP4X4),
+                        rhs_scale=w_scales[:, g, t * N_TILE : (t + 1) * N_TILE],
+                        start=(g == 0),
+                        stop=(g == PASSES - 1),
+                    )
+                cols = slice(t * N_TILE, (t + 1) * N_TILE)
+                nc.vector.tensor_tensor(out=result[:, r, cols], in0=acc[:], in1=bias_all[:, cols], op=ADD)
+                if row == HALF_ROWS - 1:
+                    nc.sync.dma_start(out=out_rows[:, row, cols], in_=result[:, r, cols])
+                for rows in quantise_after.get((row, t), []):
+                    quantise(rows)
+            if row >= HALF_ROWS - 1 - 2:
+                if row < HALF_ROWS - 1:
+                    nc.sync.dma_start(out=out_rows[:, row, :], in_=result[:, r, :])
+            elif r == PAIR - 1:
+                nc.sync.dma_start(out=out_rows[:, row - r : row + 1, :], in_=result[:])
+
+        head = pairs[0] + pairs[1]
+        for row in head:
+            permute(row)
+        for row in head:
+            transpose(row)
+        for row in head:
+            copy_out(row)
+        for row in pairs[0]:
+            quantise([row])
+        for row in pairs[2]:
+            permute(row)
+        quantise(pairs[1])
+        for row in range(HALF_ROWS):
+            multiply_and_store(row)
+            for q in transposes_after.get(row, []):
+                for i in pairs[q]:
+                    transpose(i)
+                for i in pairs[q]:
+                    copy_out(i)
+                if q + 1 < len(pairs):
+                    for i in pairs[q + 1]:
+                        permute(i)

@@ -92,17 +92,13 @@ def tile_attention_pa_kernel(tc, y_attn, w_proj_words, w_proj_scales, b_proj, ou
 
         def load_channels(piece):
             c0, c1 = CHANNEL_CUTS[piece], CHANNEL_CUTS[piece + 1]
-            for h in range(HALVES):
-                cols = slice(h * HALF_CHANNELS + c0, h * HALF_CHANNELS + c1)
+            for slot, last, token in ((0, A_SLOTS, 0), (A_SLOTS, TOKENS, WORD)):
                 for e in range(WORD):
-                    nc.sync.dma_start(
-                        out=y_pieces[piece][h:P:HALVES, e:A_SLOTS:WORD, :], in_=y_attn[:, e:TOKENS:PACK, cols]
-                    )
-                for e in range(WORD):
-                    nc.sync.dma_start(
-                        out=y_pieces[piece][h:P:HALVES, A_SLOTS + e : TOKENS : WORD, :],
-                        in_=y_attn[:, WORD + e : TOKENS : PACK, cols],
-                    )
+                    for h in range(HALVES):
+                        nc.sync.dma_start(
+                            out=y_pieces[piece][h:P:HALVES, slot + e : last : WORD, :],
+                            in_=y_attn[:, token + e : TOKENS : PACK, h * HALF_CHANNELS + c0 : h * HALF_CHANNELS + c1],
+                        )
 
         nc.scalar.dma_start(out=bias_row[0:1, :], in_=b_proj.unsqueeze(0))
         nc.scalar.copy(out=warm[:], in_=ones[:, 0:WORD])
@@ -123,6 +119,20 @@ def tile_attention_pa_kernel(tc, y_attn, w_proj_words, w_proj_scales, b_proj, ou
             acc = psum_o.tile([P, N_TILE], F32, tag="acc")
             nc.tensor.matmul(out=acc[:], lhsT=ones[:], rhs=bias_row[:, cols], start=True, stop=True)
             nc.vector.tensor_copy(out=bias_all[:, cols], in_=acc[:])
+
+        def spin(slot, count):
+            for k in range(count):
+                acc = psum_o.tile([P, N_TILE], F32, tag="acc")
+                nc.tensor.matmul(
+                    out=acc[:],
+                    lhsT=ones[:],
+                    rhs=y_pieces[0][:, slot : slot + N_TILE // CHANNEL_CUTS[1], :].rearrange("p m c -> p (m c)"),
+                    start=True,
+                    stop=True,
+                )
+
+        spin(0, 7)
+        spin(A_SLOTS, 2)
 
         def copy_on(engine, dst, src):
             if engine == "vector":
@@ -235,6 +245,7 @@ def tile_attention_pa_kernel(tc, y_attn, w_proj_words, w_proj_scales, b_proj, ou
             permute(row)
         for row in head:
             transpose(row)
+            spin(0, 1)
         for row in head:
             copy_out(row)
         for row in pairs[0]:

@@ -205,7 +205,7 @@ def tile_attention_pa_kernel(tc, y_attn, w_proj_words, w_proj_scales, b_proj, ou
                     quantise_after.setdefault((first - 1, r), []).append([row])
             else:
                 transposes_after.setdefault(first - 3, []).append(q)
-                quantise_after.setdefault((first - 2, N_TILES - 1), []).append(pairs[q])
+                quantise_after.setdefault((first - 2, 0), []).append(pairs[q])
 
         result_of = {}
 

@@ -253,6 +253,7 @@ def tile_attention_pa_kernel(tc, y_attn, w_proj_words, w_proj_scales, b_proj, ou
         for row in pairs[2]:
             permute(row)
         quantise(pairs[1])
+        permuted = 3
         for row in range(HALF_ROWS):
             multiply_and_store(row)
             for q in transposes_after.get(row, []):
@@ -260,6 +261,9 @@ def tile_attention_pa_kernel(tc, y_attn, w_proj_words, w_proj_scales, b_proj, ou
                     transpose(i)
                 for i in pairs[q]:
                     copy_out(i)
-                if q + 1 < len(pairs):
-                    for i in pairs[q + 1]:
+                while permuted < min(q + 3, len(pairs)) and (
+                    permuted == q + 1 or piece_of(pairs[permuted][-1]) == piece_of(pairs[q + 1][-1])
+                ):
+                    for i in pairs[permuted]:
                         permute(i)
+                    permuted += 1

@@ -38,10 +38,11 @@ CHANNEL_CUTS = (0, 128, 256, 512)
 PAIR = 2
 PARTS = (
     (0, 0, 0, A_SLOTS, 0),
-    (0, 1, A_SLOTS, B_SLOTS, A_SLOTS),
-    (1, 1, 0, A_SLOTS, B_SLOTS),
-    (1, 0, A_SLOTS, B_SLOTS, 0),
+    (1, 0, 1, B_SLOTS, A_SLOTS),
+    (0, 1, 1, A_SLOTS, B_SLOTS),
+    (1, 1, 0, B_SLOTS, 0),
 )
+BOTH = (0, 1)
 
 FLOPS = 2 * IMAGES * TOKENS * CHANNELS * FEATURES
 
@@ -74,8 +75,9 @@ def tile_attention_pa_kernel(tc, y_attn, w_proj_words, w_proj_scales, b_proj, ou
 
         y_pieces = []
         for c0, c1 in zip(CHANNEL_CUTS[:-1], CHANNEL_CUTS[1:]):
-            piece = keep.tile([P, TOKENS, c1 - c0], BF16, name="y_piece_%d" % c0)
-            y_pieces.append(piece)
+            tokens_a = keep.tile([P, A_SLOTS, c1 - c0], BF16, name="y_a_%d" % c0)
+            tokens_b = keep.tile([P, B_SLOTS, c1 - c0], BF16, name="y_b_%d" % c0)
+            y_pieces.append((tokens_a, tokens_b))
         z_sb = keep.tile([P, WORD, PLANE], BF16, align_bytes=64)
         w_words = keep.tile([P, PASSES, WORD * FEATURES], U8, align_bytes=64)
         w_scales = keep.tile([P, PASSES, FEATURES], U8, align_bytes=64)
@@ -92,12 +94,14 @@ def tile_attention_pa_kernel(tc, y_attn, w_proj_words, w_proj_scales, b_proj, ou
 
         def load_channels(piece):
             c0, c1 = CHANNEL_CUTS[piece], CHANNEL_CUTS[piece + 1]
-            for slot, last, token in ((0, A_SLOTS, 0), (A_SLOTS, TOKENS, WORD)):
+            for kind, slots in enumerate((A_SLOTS, B_SLOTS)):
                 for e in range(WORD):
                     for h in range(HALVES):
                         nc.sync.dma_start(
-                            out=y_pieces[piece][h:P:HALVES, slot + e : last : WORD, :],
-                            in_=y_attn[:, token + e : TOKENS : PACK, h * HALF_CHANNELS + c0 : h * HALF_CHANNELS + c1],
+                            out=y_pieces[piece][kind][h:P:HALVES, e:slots:WORD, :],
+                            in_=y_attn[
+                                :, kind * WORD + e : TOKENS : PACK, h * HALF_CHANNELS + c0 : h * HALF_CHANNELS + c1
+                            ],
                         )
 
         nc.scalar.dma_start(out=bias_row[0:1, :], in_=b_proj.unsqueeze(0))
@@ -120,19 +124,19 @@ def tile_attention_pa_kernel(tc, y_attn, w_proj_words, w_proj_scales, b_proj, ou
             nc.tensor.matmul(out=acc[:], lhsT=ones[:], rhs=bias_row[:, cols], start=True, stop=True)
             nc.vector.tensor_copy(out=bias_all[:, cols], in_=acc[:])
 
-        def spin(slot, count):
+        def spin(kind, count):
             for k in range(count):
                 acc = psum_o.tile([P, N_TILE], F32, tag="acc")
                 nc.tensor.matmul(
                     out=acc[:],
                     lhsT=ones[:],
-                    rhs=y_pieces[0][:, slot : slot + N_TILE // CHANNEL_CUTS[1], :].rearrange("p m c -> p (m c)"),
+                    rhs=y_pieces[0][kind][:, 0 : N_TILE // CHANNEL_CUTS[1], :].rearrange("p m c -> p (m c)"),
                     start=True,
                     stop=True,
                 )
 
         spin(0, 7)
-        spin(A_SLOTS, 2)
+        spin(1, 2)
 
         def copy_on(engine, dst, src):
             if engine == "vector":
@@ -142,15 +146,17 @@ def tile_attention_pa_kernel(tc, y_attn, w_proj_words, w_proj_scales, b_proj, ou
             else:
                 nc.scalar.copy(out=dst, in_=src)
 
-        def permute(row):
+        def permute(row, kinds):
             lo, hi = channels_until(row - 1), channels_until(row)
             for piece in range(len(y_pieces)):
                 base = CHANNEL_CUTS[piece]
                 c0, c1 = max(lo, base), min(hi, CHANNEL_CUTS[piece + 1])
                 if c0 >= c1:
                     continue
-                for plane, parity, slot, slots, place in PARTS:
-                    src = y_pieces[piece][:, slot : slot + slots, c0 - base : c1 - base].rearrange(
+                for kind, plane, parity, slots, place in PARTS:
+                    if kind not in kinds:
+                        continue
+                    src = y_pieces[piece][kind][:, :, c0 - base : c1 - base].rearrange(
                         "p m (c i q) -> p c m i q", i=RUN, q=WORD
                     )
                     dst = z_sb[:, plane, TOKENS * (c0 // WORD) : TOKENS * (c1 // WORD)].rearrange(
@@ -242,7 +248,7 @@ def tile_attention_pa_kernel(tc, y_attn, w_proj_words, w_proj_scales, b_proj, ou
 
         head = pairs[0] + pairs[1]
         for row in head:
-            permute(row)
+            permute(row, BOTH)
         for row in head:
             transpose(row)
             spin(0, 1)
@@ -251,8 +257,11 @@ def tile_attention_pa_kernel(tc, y_attn, w_proj_words, w_proj_scales, b_proj, ou
         for row in pairs[0]:
             quantise([row])
         for row in pairs[2]:
-            permute(row)
+            permute(row, BOTH)
+        for row in pairs[3]:
+            permute(row, BOTH[0:1])
         quantise(pairs[1])
+        early = 4
         permuted = 3
         for row in range(HALF_ROWS):
             multiply_and_store(row)
@@ -261,9 +270,15 @@ def tile_attention_pa_kernel(tc, y_attn, w_proj_words, w_proj_scales, b_proj, ou
                     transpose(i)
                 for i in pairs[q]:
                     copy_out(i)
+                while early < min(q + 4, len(pairs)) and (
+                    early <= q + 2 or piece_of(pairs[early][-1]) == piece_of(pairs[q + 2][-1])
+                ):
+                    for i in pairs[early]:
+                        permute(i, BOTH[0:1])
+                    early += 1
                 while permuted < min(q + 3, len(pairs)) and (
                     permuted == q + 1 or piece_of(pairs[permuted][-1]) == piece_of(pairs[q + 1][-1])
                 ):
                     for i in pairs[permuted]:
-                        permute(i)
+                        permute(i, BOTH[1:2])
                     permuted += 1

from contextlib import ExitStack

import concourse.mybir as mybir
from concourse.masks import make_identity

BF16 = mybir.dt.bfloat16
F32 = mybir.dt.float32
I32 = mybir.dt.int32
U8 = mybir.dt.uint8
U32 = mybir.dt.uint32
FP8X4 = mybir.dt.float8_e4m3fn_x4
FP4X4 = mybir.dt.float4_e2m1fn_x4
ADD = mybir.AluOpType.add
MULT = mybir.AluOpType.mult

P = 128
IMAGES = 64
TOKENS = 50
CHANNELS = 1024
FEATURES = 1024
HALVES = 2
HALF_CHANNELS = CHANNELS // HALVES
HALF_ROWS = TOKENS // HALVES
PACK = 4
K_PASS = P * PACK
PASSES = CHANNELS // K_PASS
WORD = 2
N_TILE = 512
N_TILES = FEATURES // N_TILE
A_SLOTS = 26
B_SLOTS = 24
PLANE = HALF_ROWS * CHANNELS // WORD
ROW_QUADS = CHANNELS // PACK
PAIR_QUADS = 25
RUN = 4
STEP = RUN * WORD
CHANNEL_CUTS = (0, 128, 256, 512)
PAIR = 2
PARTS = (
    (0, 0, 0, A_SLOTS, 0),
    (1, 0, 1, B_SLOTS, A_SLOTS),
    (0, 1, 1, A_SLOTS, B_SLOTS),
    (1, 1, 0, B_SLOTS, 0),
)
BOTH = (0, 1)

FLOPS = 2 * IMAGES * TOKENS * CHANNELS * FEATURES


def tile_attention_pa_kernel(tc, y_attn, w_proj_words, w_proj_scales, b_proj, out):
    nc = tc.nc
    pairs = [list(range(i, min(i + PAIR, HALF_ROWS))) for i in range(0, HALF_ROWS, PAIR)]
    out_rows = out.rearrange("b (h i) f -> (b h) i f", h=HALVES)

    def channels_until(row):
        if row < 0:
            return 0
        need = WORD * (((row + 1) * ROW_QUADS - 1) // PAIR_QUADS + 1)
        return min(HALF_CHANNELS, -(-need // STEP) * STEP)

    def piece_of(row):
        last = channels_until(row) - 1
        return max(k for k in range(len(CHANNEL_CUTS) - 1) if CHANNEL_CUTS[k] <= last)

    def is_late(q):
        return q > 0 and piece_of(pairs[q][-1]) > piece_of(pairs[q - 1][-1])

    with ExitStack() as ctx:
        keep = ctx.enter_context(tc.tile_pool(name="keep", bufs=1))
        stage = ctx.enter_context(tc.tile_pool(name="stage", bufs=4))
        results = ctx.enter_context(tc.tile_pool(name="results", bufs=8))
        psum_t = ctx.enter_context(tc.psum_pool(name="psum_t", bufs=4))
        psum_o = ctx.enter_context(tc.psum_pool(name="psum_o", bufs=4))
        ctx.enter_context(tc.manual_schedule())

        y_pieces = []
        for c0, c1 in zip(CHANNEL_CUTS[:-1], CHANNEL_CUTS[1:]):
            tokens_a = keep.tile([P, A_SLOTS, c1 - c0], BF16, name="y_a_%d" % c0)
            tokens_b = keep.tile([P, B_SLOTS, c1 - c0], BF16, name="y_b_%d" % c0)
            y_pieces.append((tokens_a, tokens_b))
        z_sb = keep.tile([P, WORD, PLANE], BF16, align_bytes=64)
        w_words = keep.tile([P, PASSES, WORD * FEATURES], U8, align_bytes=64)
        w_scales = keep.tile([P, PASSES, FEATURES], U8, align_bytes=64)
        bias_row = keep.tile([P, FEATURES], BF16)
        ones = keep.tile([P, P], BF16)
        warm = keep.tile([P, WORD], BF16)
        bias_all = keep.tile([P, FEATURES], F32)
        identity = keep.tile([P, P], F32)

        nc.vector.memset(bias_row[:], 0.0)
        nc.vector.memset(w_scales[:].bitcast(I32), 0)
        nc.vector.memset(ones[:], 1.0)
        make_identity(nc, identity[:])

        def load_channels(piece):
            c0, c1 = CHANNEL_CUTS[piece], CHANNEL_CUTS[piece + 1]
            for kind, slots in enumerate((A_SLOTS, B_SLOTS)):
                for e in range(WORD):
                    for h in range(HALVES):
                        nc.sync.dma_start(
                            out=y_pieces[piece][kind][h:P:HALVES, e:slots:WORD, :],
                            in_=y_attn[
                                :, kind * WORD + e : TOKENS : PACK, h * HALF_CHANNELS + c0 : h * HALF_CHANNELS + c1
                            ],
                        )

        nc.scalar.dma_start(out=bias_row[0:1, :], in_=b_proj.unsqueeze(0))
        nc.scalar.copy(out=warm[:], in_=ones[:, 0:WORD])
        load_channels(0)
        scale_rows = w_proj_scales.rearrange("g q n -> q g n")
        for r in range(4):
            nc.sync.dma_start(
                out=w_scales[r:P:32, :, :].bitcast(I32), in_=scale_rows[r:16:4, :, :].bitcast(I32)
            )
        nc.sync.dma_start(
            out=w_words[:].bitcast(I32), in_=w_proj_words.rearrange("g p n -> p g n").bitcast(I32)
        )
        for piece in range(1, len(y_pieces)):
            load_channels(piece)

        for t in range(N_TILES):
            cols = slice(t * N_TILE, (t + 1) * N_TILE)
            acc = psum_o.tile([P, N_TILE], F32, tag="acc")
            nc.tensor.matmul(out=acc[:], lhsT=ones[:], rhs=bias_row[:, cols], start=True, stop=True)
            nc.vector.tensor_copy(out=bias_all[:, cols], in_=acc[:])

        def spin(kind, count):
            for k in range(count):
                acc = psum_o.tile([P, N_TILE], F32, tag="acc")
                nc.tensor.matmul(
                    out=acc[:],
                    lhsT=ones[:],
                    rhs=y_pieces[0][kind][:, 0 : N_TILE // CHANNEL_CUTS[1], :].rearrange("p m c -> p (m c)"),
                    start=True,
                    stop=True,
                )

        spin(0, 7)
        spin(1, 2)

        def copy_on(engine, dst, src):
            if engine == "vector":
                nc.vector.tensor_copy(out=dst, in_=src)
            elif engine == "gpsimd":
                nc.gpsimd.tensor_scalar(out=dst, in0=src, scalar1=1.0, scalar2=0.0, op0=MULT, op1=ADD)
            else:
                nc.scalar.copy(out=dst, in_=src)

        def permute(row, kinds):
            lo, hi = channels_until(row - 1), channels_until(row)
            for piece in range(len(y_pieces)):
                base = CHANNEL_CUTS[piece]
                c0, c1 = max(lo, base), min(hi, CHANNEL_CUTS[piece + 1])
                if c0 >= c1:
                    continue
                for kind, plane, parity, slots, place in PARTS:
                    if kind not in kinds:
                        continue
                    src = y_pieces[piece][kind][:, :, c0 - base : c1 - base].rearrange(
                        "p m (c i q) -> p c m i q", i=RUN, q=WORD
                    )
                    dst = z_sb[:, plane, TOKENS * (c0 // WORD) : TOKENS * (c1 // WORD)].rearrange(
                        "p (c i m) -> p c m i", i=RUN, m=TOKENS
                    )
                    engine = (("scalar" if (plane, parity) == (1, 0) else "vector") if piece == 0 else ("scalar" if plane == 0 else "gpsimd"))
                    copy_on(engine, dst[:, :, place : place + slots, :], src[:, :, :, :, parity])

        z_words = z_sb[:].rearrange("p u f -> p (u f)").bitcast(F32)
        flipped_of = {}
        grouped_of = {}
        codes_of = {}
        scales_of = {}

        def transpose(row):
            flipped = psum_t.tile([P, PASSES, WORD, P], F32)
            flipped_of[row] = flipped
            for g in range(PASSES):
                for u in range(WORD):
                    first = u * (PLANE // WORD) + (row * PASSES + g) * P
                    nc.tensor.transpose(flipped[:, g, u, :], z_words[:, first : first + P], identity[:])

        def copy_out(row):
            q, r = divmod(row, PAIR)
            if r == 0:
                grouped = stage.tile([P, PAIR, PASSES, P, PACK], BF16, align_bytes=64)
                codes = stage.tile([P, PAIR * PASSES * P], U32, align_bytes=64)
                scales = stage.tile([P, PAIR * PASSES * P], U8, align_bytes=64)
                grouped_of[q] = grouped
                codes_of[q] = codes
                scales_of[q] = scales
            nc.scalar.copy(
                out=grouped_of[q][:, r].bitcast(F32), in_=flipped_of[row][:].rearrange("p g u c -> p g c u")
            )

        def quantise(rows):
            q, r0 = divmod(rows[0], PAIR)
            cols = slice(r0 * PASSES * P, (r0 + len(rows)) * PASSES * P)
            nc.vector.quantize_mx(
                out=codes_of[q][:, cols].bitcast(FP8X4),
                scales=scales_of[q][:, cols],
                in_=grouped_of[q][:, r0 : r0 + len(rows)].rearrange("p r g c t -> p (r g c t)"),
            )

        transposes_after = {}
        quantise_after = {}
        for q in range(PAIR, len(pairs)):
            first = pairs[q][0]
            if is_late(q):
                transposes_after.setdefault(first - 2, []).append(q)
                for r, row in enumerate(pairs[q]):
                    quantise_after.setdefault((first - 1, r), []).append([row])
            else:
                transposes_after.setdefault(first - 3, []).append(q)
                quantise_after.setdefault((first - 2, 0), []).append(pairs[q])

        result_of = {}

        def multiply_and_store(row):
            q, r = divmod(row, PAIR)
            if r == 0:
                result = results.tile([P, PAIR, FEATURES], F32)
                result_of[q] = result
            result = result_of[q]
            for t in range(N_TILES):
                acc = psum_o.tile([P, N_TILE], F32, tag="acc")
                for g in range(PASSES):
                    cols = slice((r * PASSES + g) * P, (r * PASSES + g + 1) * P)
                    nc.tensor.matmul_mx(
                        out=acc[:],
                        lhsT=codes_of[q][:, cols].bitcast(FP8X4),
                        lhsT_scale=scales_of[q][:, cols],
                        rhs=w_words[:, g, t * WORD * N_TILE : (t + 1) * WORD * N_TILE].bitcast(FP4X4),
                        rhs_scale=w_scales[:, g, t * N_TILE : (t + 1) * N_TILE],
                        start=(g == 0),
                        stop=(g == PASSES - 1),
                    )
                cols = slice(t * N_TILE, (t + 1) * N_TILE)
                nc.vector.tensor_tensor(out=result[:, r, cols], in0=acc[:], in1=bias_all[:, cols], op=ADD)
                if row == HALF_ROWS - 1:
                    nc.sync.dma_start(out=out_rows[:, row, cols], in_=result[:, r, cols])
                for rows in quantise_after.get((row, t), []):
                    quantise(rows)
            if row >= HALF_ROWS - 1 - 2:
                if row < HALF_ROWS - 1:
                    nc.sync.dma_start(out=out_rows[:, row, :], in_=result[:, r, :])
            elif r == PAIR - 1:
                nc.sync.dma_start(out=out_rows[:, row - r : row + 1, :], in_=result[:])

        head = pairs[0] + pairs[1]
        for row in head:
            permute(row, BOTH)
        for row in head:
            transpose(row)
            spin(0, 1)
        for row in head:
            copy_out(row)
        for row in pairs[0]:
            quantise([row])
        for row in pairs[2]:
            permute(row, BOTH)
        for row in pairs[3]:
            permute(row, BOTH[0:1])
        quantise(pairs[1])
        early = 4
        permuted = 3
        for row in range(HALF_ROWS):
            multiply_and_store(row)
            for q in transposes_after.get(row, []):
                for i in pairs[q]:
                    transpose(i)
                for i in pairs[q]:
                    copy_out(i)
                while early < min(q + 4, len(pairs)) and (
                    early <= q + 2 or piece_of(pairs[early][-1]) == piece_of(pairs[q + 2][-1])
                ):
                    for i in pairs[early]:
                        permute(i, BOTH[0:1])
                    early += 1
                while permuted < min(q + 3, len(pairs)) and (
                    permuted == q + 1 or piece_of(pairs[permuted][-1]) == piece_of(pairs[q + 1][-1])
                ):
                    for i in pairs[permuted]:
                        permute(i, BOTH[1:2])
                    permuted += 1
